import numpy as np
import ml_dtypes


def mxq(x, axis, fmt="e4m3"):
    dtype, down = {"e4m3": (ml_dtypes.float8_e4m3fn, 7), "e5m2": (ml_dtypes.float8_e5m2, 14)}[fmt]
    v = np.moveaxis(np.asarray(x, np.float32).astype(ml_dtypes.bfloat16).astype(np.float64), axis, -1)
    blocks = v.reshape(v.shape[:-1] + (-1, 32))
    amax = np.abs(blocks).max(-1, keepdims=True)
    byte = np.maximum(np.where(amax > 0, np.frexp(amax)[1] - 1 + 127, 0) - down, 1)
    scale = np.exp2(byte - 127.0)
    codes = (blocks / scale).astype(np.float32).astype(dtype).astype(np.float64)
    return np.moveaxis((codes * scale).reshape(v.shape), -1, axis)


WIDE = False


def mx_kscale(k):
    if not WIDE:
        return np.ones(k)
    levels = np.array([10, -10, 5, -5, 0])
    a = np.random.permutation(np.resize(levels, k // 512 * 4)).reshape(k // 512, 4)
    idx = np.arange(k)
    return np.exp2(a[idx // 512, idx % 128 // 32])


BF16 = ml_dtypes.bfloat16


def bf(x):
    return np.asarray(x, np.float32).astype(BF16)


def f64(x):
    return np.asarray(x).astype(np.float64)


NT, N, C_IN, C_H, C_OUT, ORDER = 2048, 2048, 1024, 512, 256, 3


def setup_inputs():
    s = mx_kscale(C_IN)
    return {"nf_mats": bf(np.random.standard_normal((N, C_IN)) * s),
            "conv_mats": bf(np.random.standard_normal((NT, N)) / np.sqrt(N)),
            "W1": bf(np.random.standard_normal((C_IN, C_H)) / np.sqrt(C_IN) / s[:, None]),
            "b1": bf(np.random.standard_normal(C_H) * 0.2),
            "c1": bf(0.4 ** np.arange(ORDER) * (1.0 + 0.1 * np.random.standard_normal(ORDER)))}


def reference(nf_mats, conv_mats, W1, b1, c1):
    coeffs = f64(c1)
    h = (mxq(f64(nf_mats), 1, "e4m3") @ mxq(f64(W1), 0, "e4m3")) + f64(b1)
    z = mxq(f64(conv_mats), 1, "e4m3") @ mxq(h, 0, "e4m3")
    p = z
    acc = coeffs[0] * z
    for d in range(1, ORDER):
        p = p * z
        acc = acc + coeffs[d] * p
    return acc

@@ -1,0 +1,211 @@
+from contextlib import ExitStack
+
+import concourse.mybir as mybir
+from concourse.masks import make_identity
+
+F32 = mybir.dt.float32
+BF16 = mybir.dt.bfloat16
+U32 = mybir.dt.uint32
+U8 = mybir.dt.uint8
+FP8X4 = mybir.dt.float8_e4m3fn_x4
+ALU = mybir.AluOpType
+ACT = mybir.ActivationFunctionType
+
+P = 128
+NT, N, C_IN, C_H = 2048, 2048, 1024, 512
+FLOPS = 2 * N * C_IN * C_H + 2 * NT * N * C_H
+
+LOOKAHEAD = 3
+
+
+def tile_sketchgcn_pa_kernel(tc, nf_mats, conv_mats, W1, b1, c1, out):
+    nc = tc.nc
+    with ExitStack() as ctx:
+        const = ctx.enter_context(tc.tile_pool(name="const", bufs=1))
+        nf_pool = ctx.enter_context(tc.tile_pool(name="nf_raw", bufs=8))
+        cv_pool = ctx.enter_context(tc.tile_pool(name="cv_raw", bufs=6))
+        nfg_pool = ctx.enter_context(tc.tile_pool(name="nf_grouped", bufs=2))
+        nfc_pool = ctx.enter_context(tc.tile_pool(name="nf_codes", bufs=2))
+        hg_pool = ctx.enter_context(tc.tile_pool(name="h_grouped", bufs=2))
+        cvg_pool = ctx.enter_context(tc.tile_pool(name="cv_grouped", bufs=3))
+        cvc_pool = ctx.enter_context(tc.tile_pool(name="cv_codes", bufs=4))
+        poly_pool = ctx.enter_context(tc.tile_pool(name="poly", bufs=4))
+        res_pool = ctx.enter_context(tc.tile_pool(name="res", bufs=3))
+        ps_t = ctx.enter_context(tc.psum_pool(name="ps_t", bufs=4))
+        ps_m = ctx.enter_context(tc.psum_pool(name="ps_m", bufs=4))
+        ctx.enter_context(tc.manual_schedule())
+
+        ident = const.tile([P, P], F32)
+        make_identity(nc, ident[:])
+        row = const.tile([P, C_H + 32], BF16)
+        nc.vector.memset(row[:], 0.0)
+        ones = const.tile([P, P], BF16)
+        nc.vector.memset(ones[:], 1.0)
+        nc.scalar.dma_start(out=row[0:1, 0:C_H], in_=b1.rearrange("(o c) -> o c", o=1))
+        nc.scalar.dma_start(out=row[0:1, C_H : C_H + 3], in_=c1.rearrange("(o c) -> o c", o=1))
+
+        w1_raw = const.tile([P, 8, C_H], BF16)
+        for half in range(2):
+            nc.sync.dma_start(
+                out=w1_raw[:, 4 * half : 4 * half + 4, :].rearrange("q (u e) c -> q u e c", u=2),
+                in_=W1[512 * half : 512 * half + 512, :].rearrange("(u q e) c -> q u e c", u=2, e=2),
+            )
+        nf_raw = []
+        for r in range(8):
+            nfr = nf_pool.tile([P, 2 * C_IN], BF16, tag="nfr")
+            nc.sync.dma_start(
+                out=nfr[:].rearrange("j (e k) -> j e k", e=2),
+                in_=nf_mats[256 * r : 256 * r + 256, :].rearrange("(j e) k -> j e k", e=2),
+            )
+            nf_raw.append(nfr)
+        cv_raw = []
+        for i in range(8):
+            cvr = cv_pool.tile([P, 2 * N], BF16, tag="cvr")
+            nc.sync.dma_start(
+                out=cvr[:].rearrange("p (a n) -> p a n", a=2),
+                in_=conv_mats[256 * i : 256 * i + 256, :].rearrange("(p a) n -> p a n", a=2),
+            )
+            cv_raw.append(cvr)
+
+        w1_grouped = const.tile([P, 2, C_H, 4], BF16, align_bytes=64)
+        w1_codes = const.tile([P, 2 * C_H], U32, align_bytes=64)
+        w1_scales = const.tile([P, 2 * C_H], U8, align_bytes=64)
+        for half in range(2):
+            nc.vector.tensor_copy(
+                out=w1_grouped[:, half, :, :].rearrange("p (c i) t -> p c t i", i=4),
+                in_=w1_raw[:, 4 * half : 4 * half + 4, :].rearrange("p t (c i) -> p c t i", i=4),
+            )
+        nc.vector.quantize_mx(
+            out=w1_codes[:].bitcast(FP8X4),
+            scales=w1_scales[:],
+            in_=w1_grouped[:].rearrange("p h c t -> p (h c t)"),
+        )
+        bias = const.tile([P, C_H], F32)
+        coef = const.tile([P, 32], F32)
+
+        h_codes = const.tile([P, 4 * C_H], U32, align_bytes=64)
+        h_scales = const.tile([P, 4 * C_H], U8, align_bytes=64)
+
+        def front(raw_words, grouped_pool, codes_pool, tag):
+            grouped = grouped_pool.tile([P, 4096], BF16, tag=tag + "g", align_bytes=64)
+            g32 = grouped[:].bitcast(F32)
+            banks = []
+            for b in range(4):
+                tp = ps_t.tile([P, 512], F32, tag="tp")
+                for s in range(4):
+                    nc.tensor.transpose(out=tp[:, 128 * s : 128 * s + 128], in_=raw_words[b][s], identity=ident[:])
+                banks.append(tp)
+            for b in range(4):
+                nc.scalar.copy(
+                    out=g32[:, 512 * b : 512 * b + 512].rearrange("p (a j u) -> p a j u", a=2, u=2),
+                    in_=banks[b][:].rearrange("p (a u j) -> p a j u", a=2, u=2),
+                )
+            codes = codes_pool.tile([P, 1024], U32, tag=tag + "c", align_bytes=64)
+            scales = codes_pool.tile([P, 1024], U8, tag=tag + "s", align_bytes=64)
+            nc.vector.quantize_mx(out=codes[:].bitcast(FP8X4), scales=scales[:], in_=grouped[:])
+            return codes, scales
+
+        def front_nf(g):
+            words = []
+            for ue in range(4):
+                src = nf_raw[2 * g + ue // 2][:].bitcast(F32)
+                base = 512 * (ue % 2)
+                words.append([src[:, base + 128 * s : base + 128 * s + 128] for s in range(4)])
+            return front(words, nfg_pool, nfc_pool, "nf")
+
+        def front_cv(i):
+            src = cv_raw[i][:].bitcast(F32)
+            words = [[src[:, 512 * b + 128 * s : 512 * b + 128 * s + 128] for s in range(4)] for b in range(4)]
+            return front(words, cvg_pool, cvc_pool, "cv")
+
+        def back_nf(nf_q):
+            codes, scales = nf_q
+            hg = hg_pool.tile([P, 4 * C_H], BF16, tag="hg", align_bytes=64)
+            for cb in range(4):
+                acc = ps_m.tile([P, 512], F32, tag="mm")
+                for ue in range(4):
+                    for kp in range(2):
+                        m_cols = slice(128 * (2 * ue + kp), 128 * (2 * ue + kp) + 128)
+                        n_cols = slice(512 * kp + 128 * cb, 512 * kp + 128 * cb + 128)
+                        nc.tensor.matmul_mx(
+                            out=acc[:, 128 * ue : 128 * ue + 128],
+                            lhsT=codes[:, m_cols].bitcast(FP8X4),
+                            lhsT_scale=scales[:, m_cols],
+                            rhs=w1_codes[:, n_cols].bitcast(FP8X4),
+                            rhs_scale=w1_scales[:, n_cols],
+                            start=(kp == 0),
+                            stop=(kp == 1),
+                        )
+                nc.vector.tensor_tensor(
+                    out=hg[:, 512 * cb : 512 * cb + 512].rearrange("p (c t) -> p c t", t=4),
+                    in0=acc[:].rearrange("p (t c) -> p c t", t=4),
+                    in1=bias[:, 128 * cb : 128 * cb + 128].unsqueeze(2).to_broadcast([P, 128, 4]),
+                    op=ALU.add,
+                )
+            return hg
+
+        def quant_h(g, hg):
+            cols = slice(C_H * g, C_H * g + C_H)
+            nc.vector.quantize_mx(out=h_codes[:, cols].bitcast(FP8X4), scales=h_scales[:, cols], in_=hg[:])
+
+        def back_cv(i, cv_q):
+            codes, scales = cv_q
+            zs = []
+            for a in range(2):
+                z = ps_m.tile([P, 512], F32, tag="mm")
+                for g in range(4):
+                    m_cols = slice(128 * (4 * a + g), 128 * (4 * a + g) + 128)
+                    n_cols = slice(C_H * g, C_H * g + C_H)
+                    nc.tensor.matmul_mx(
+                        out=z[:],
+                        lhsT=codes[:, m_cols].bitcast(FP8X4),
+                        lhsT_scale=scales[:, m_cols],
+                        rhs=h_codes[:, n_cols].bitcast(FP8X4),
+                        rhs_scale=h_scales[:, n_cols],
+                        start=(g == 0),
+                        stop=(g == 3),
+                    )
+                zs.append(z)
+            ts = []
+            for a in range(2):
+                t = poly_pool.tile([P, 512], F32, tag="t")
+                nc.scalar.activation(out=t[:], in_=zs[a][:], func=ACT.Identity, bias=coef[:, 1:2], scale=coef[:, 2:3])
+                ts.append(t)
+            for a in range(2):
+                nc.vector.tensor_tensor(out=ts[a][:], in0=ts[a][:], in1=zs[a][:], op=ALU.mult)
+            res = res_pool.tile([P, 2, C_H], F32, tag="res")
+            for a in range(2):
+                nc.vector.scalar_tensor_tensor(
+                    out=res[:, a, :], in0=ts[a][:], scalar=coef[:, 0:1], in1=zs[a][:], op0=ALU.add, op1=ALU.mult
+                )
+            nc.sync.dma_start(out=out[256 * i : 256 * i + 256, :].rearrange("(p a) c -> p a c", a=2), in_=res[:])
+
+        nf_q = {}
+        cv_q = {}
+        hgs = {}
+        nf_q[0] = front_nf(0)
+        nf_q[1] = front_nf(1)
+        bias_ps = ps_m.tile([P, 512], F32, tag="mm")
+        nc.tensor.matmul(out=bias_ps[:], lhsT=ones[:], rhs=row[:, 0:C_H], start=True, stop=True)
+        coef_ps = ps_m.tile([P, 512], F32, tag="mm")
+        nc.tensor.matmul(out=coef_ps[:, 0:32], lhsT=ones[:], rhs=row[:, C_H : C_H + 32], start=True, stop=True)
+        nc.vector.tensor_copy(out=bias[:], in_=bias_ps[:])
+        nc.vector.tensor_copy(out=coef[:], in_=coef_ps[:, 0:32])
+        hgs[0] = back_nf(nf_q[0])
+        nf_q[2] = front_nf(2)
+        quant_h(0, hgs[0])
+        hgs[1] = back_nf(nf_q[1])
+        nf_q[3] = front_nf(3)
+        quant_h(1, hgs[1])
+        hgs[2] = back_nf(nf_q[2])
+        cv_q[0] = front_cv(0)
+        quant_h(2, hgs[2])
+        hgs[3] = back_nf(nf_q[3])
+        cv_q[1] = front_cv(1)
+        quant_h(3, hgs[3])
+        for i in range(2, LOOKAHEAD):
+            cv_q[i] = front_cv(i)
+        for i in range(8):
+            back_cv(i, cv_q[i])
+            if i + LOOKAHEAD < 8:
+                cv_q[i + LOOKAHEAD] = front_cv(i + LOOKAHEAD)

@@ -86,7 +86,7 @@ def tile_sketchgcn_pa_kernel(tc, nf_mats, conv_mats, W1, b1, c1, out):
         h_codes = const.tile([P, 4 * C_H], U32, align_bytes=64)
         h_scales = const.tile([P, 4 * C_H], U8, align_bytes=64)
 
-        def front(raw_words, grouped_pool, codes_pool, tag):
+        def front(raw_words, grouped_pool, tag):
             grouped = grouped_pool.tile([P, 4096], BF16, tag=tag + "g", align_bytes=64)
             g32 = grouped[:].bitcast(F32)
             banks = []
@@ -100,6 +100,9 @@ def tile_sketchgcn_pa_kernel(tc, nf_mats, conv_mats, W1, b1, c1, out):
                     out=g32[:, 512 * b : 512 * b + 512].rearrange("p (a j u) -> p a j u", a=2, u=2),
                     in_=banks[b][:].rearrange("p (a u j) -> p a j u", a=2, u=2),
                 )
+            return grouped
+
+        def quantise(grouped, codes_pool, tag):
             codes = codes_pool.tile([P, 1024], U32, tag=tag + "c", align_bytes=64)
             scales = codes_pool.tile([P, 1024], U8, tag=tag + "s", align_bytes=64)
             nc.vector.quantize_mx(out=codes[:].bitcast(FP8X4), scales=scales[:], in_=grouped[:])
@@ -111,12 +114,12 @@ def tile_sketchgcn_pa_kernel(tc, nf_mats, conv_mats, W1, b1, c1, out):
                 src = nf_raw[2 * g + ue // 2][:].bitcast(F32)
                 base = 512 * (ue % 2)
                 words.append([src[:, base + 128 * s : base + 128 * s + 128] for s in range(4)])
-            return front(words, nfg_pool, nfc_pool, "nf")
+            return front(words, nfg_pool, "nf")
 
         def front_cv(i):
             src = cv_raw[i][:].bitcast(F32)
             words = [[src[:, 512 * b + 128 * s : 512 * b + 128 * s + 128] for s in range(4)] for b in range(4)]
-            return front(words, cvg_pool, cvc_pool, "cv")
+            return front(words, cvg_pool, "cv")
 
         def back_nf(nf_q):
             codes, scales = nf_q
@@ -171,20 +174,37 @@ def tile_sketchgcn_pa_kernel(tc, nf_mats, conv_mats, W1, b1, c1, out):
                 t = poly_pool.tile([P, 512], F32, tag="t")
                 nc.scalar.activation(out=t[:], in_=zs[a][:], func=ACT.Identity, bias=coef[:, 1:2], scale=coef[:, 2:3])
                 ts.append(t)
-            for a in range(2):
-                nc.vector.tensor_tensor(out=ts[a][:], in0=ts[a][:], in1=zs[a][:], op=ALU.mult)
             res = res_pool.tile([P, 2, C_H], F32, tag="res")
-            for a in range(2):
+            out_rows = out[256 * i : 256 * i + 256, :].rearrange("(p a) c -> p a c", a=2)
+
+            def second(a):
+                nc.vector.tensor_tensor(out=ts[a][:], in0=ts[a][:], in1=zs[a][:], op=ALU.mult)
+
+            def third(a):
                 nc.vector.scalar_tensor_tensor(
                     out=res[:, a, :], in0=ts[a][:], scalar=coef[:, 0:1], in1=zs[a][:], op0=ALU.add, op1=ALU.mult
                 )
-            nc.sync.dma_start(out=out[256 * i : 256 * i + 256, :].rearrange("(p a) c -> p a c", a=2), in_=res[:])
 
+            if i < 7:
+                second(0)
+                second(1)
+                third(0)
+                third(1)
+                nc.sync.dma_start(out=out_rows, in_=res[:])
+            else:
+                for a in range(2):
+                    second(a)
+                    third(a)
+                    nc.sync.dma_start(out=out_rows[:, a, :], in_=res[:, a, :])
+
+        nf_g = {}
         nf_q = {}
+        cv_g = {}
         cv_q = {}
         hgs = {}
-        nf_q[0] = front_nf(0)
-        nf_q[1] = front_nf(1)
+        nf_g[0] = front_nf(0)
+        nf_q[0] = quantise(nf_g[0], nfc_pool, "nf")
+        nf_g[1] = front_nf(1)
         bias_ps = ps_m.tile([P, 512], F32, tag="mm")
         nc.tensor.matmul(out=bias_ps[:], lhsT=ones[:], rhs=row[:, 0:C_H], start=True, stop=True)
         coef_ps = ps_m.tile([P, 512], F32, tag="mm")
@@ -192,20 +212,27 @@ def tile_sketchgcn_pa_kernel(tc, nf_mats, conv_mats, W1, b1, c1, out):
         nc.vector.tensor_copy(out=bias[:], in_=bias_ps[:])
         nc.vector.tensor_copy(out=coef[:], in_=coef_ps[:, 0:32])
         hgs[0] = back_nf(nf_q[0])
-        nf_q[2] = front_nf(2)
+        nf_q[1] = quantise(nf_g[1], nfc_pool, "nf")
         quant_h(0, hgs[0])
+        nf_g[2] = front_nf(2)
+        nf_q[2] = quantise(nf_g[2], nfc_pool, "nf")
+        nf_g[3] = front_nf(3)
         hgs[1] = back_nf(nf_q[1])
-        nf_q[3] = front_nf(3)
+        nf_q[3] = quantise(nf_g[3], nfc_pool, "nf")
         quant_h(1, hgs[1])
+        cv_g[0] = front_cv(0)
         hgs[2] = back_nf(nf_q[2])
-        cv_q[0] = front_cv(0)
-        quant_h(2, hgs[2])
+        cv_q[0] = quantise(cv_g[0], cvc_pool, "cv")
+        cv_g[1] = front_cv(1)
         hgs[3] = back_nf(nf_q[3])
-        cv_q[1] = front_cv(1)
+        quant_h(2, hgs[2])
         quant_h(3, hgs[3])
+        cv_q[1] = quantise(cv_g[1], cvc_pool, "cv")
         for i in range(2, LOOKAHEAD):
-            cv_q[i] = front_cv(i)
+            cv_g[i] = front_cv(i)
+            cv_q[i] = quantise(cv_g[i], cvc_pool, "cv")
         for i in range(8):
             back_cv(i, cv_q[i])
             if i + LOOKAHEAD < 8:
-                cv_q[i + LOOKAHEAD] = front_cv(i + LOOKAHEAD)
+                cv_g[i + LOOKAHEAD] = front_cv(i + LOOKAHEAD)
+                cv_q[i + LOOKAHEAD] = quantise(cv_g[i + LOOKAHEAD], cvc_pool, "cv")

@@ -16,6 +16,7 @@ NT, N, C_IN, C_H = 2048, 2048, 1024, 512
 FLOPS = 2 * N * C_IN * C_H + 2 * NT * N * C_H
 
 LOOKAHEAD = 3
+GPSIMD_TILES = ((1, 1), (3, 1), (5, 1))
 
 
 def tile_sketchgcn_pa_kernel(tc, nf_mats, conv_mats, W1, b1, c1, out):
@@ -30,7 +31,8 @@ def tile_sketchgcn_pa_kernel(tc, nf_mats, conv_mats, W1, b1, c1, out):
         cvg_pool = ctx.enter_context(tc.tile_pool(name="cv_grouped", bufs=3))
         cvc_pool = ctx.enter_context(tc.tile_pool(name="cv_codes", bufs=4))
         poly_pool = ctx.enter_context(tc.tile_pool(name="poly", bufs=4))
-        res_pool = ctx.enter_context(tc.tile_pool(name="res", bufs=3))
+        gp_pool = ctx.enter_context(tc.tile_pool(name="gp", bufs=2))
+        res_pool = ctx.enter_context(tc.tile_pool(name="res", bufs=4))
         ps_t = ctx.enter_context(tc.psum_pool(name="ps_t", bufs=4))
         ps_m = ctx.enter_context(tc.psum_pool(name="ps_m", bufs=4))
         ctx.enter_context(tc.manual_schedule())
@@ -41,6 +43,8 @@ def tile_sketchgcn_pa_kernel(tc, nf_mats, conv_mats, W1, b1, c1, out):
         nc.vector.memset(row[:], 0.0)
         ones = const.tile([P, P], BF16)
         nc.vector.memset(ones[:], 1.0)
+        unit = const.tile([P, 1], F32)
+        nc.vector.memset(unit[:], 1.0)
         nc.scalar.dma_start(out=row[0:1, 0:C_H], in_=b1.rearrange("(o c) -> o c", o=1))
         nc.scalar.dma_start(out=row[0:1, C_H : C_H + 3], in_=c1.rearrange("(o c) -> o c", o=1))
 
@@ -169,13 +173,29 @@ def tile_sketchgcn_pa_kernel(tc, nf_mats, conv_mats, W1, b1, c1, out):
                         stop=(g == 3),
                     )
                 zs.append(z)
-            ts = []
-            for a in range(2):
-                t = poly_pool.tile([P, 512], F32, tag="t")
-                nc.scalar.activation(out=t[:], in_=zs[a][:], func=ACT.Identity, bias=coef[:, 1:2], scale=coef[:, 2:3])
-                ts.append(t)
             res = res_pool.tile([P, 2, C_H], F32, tag="res")
             out_rows = out[256 * i : 256 * i + 256, :].rearrange("(p a) c -> p a c", a=2)
+            on_gpsimd = [(i, a) in GPSIMD_TILES for a in range(2)]
+            ts = {}
+            for a in range(2):
+                if on_gpsimd[a]:
+                    zc = gp_pool.tile([P, 512], F32, tag="zc")
+                    nc.scalar.copy(out=zc[:], in_=zs[a][:])
+                    tg = gp_pool.tile([P, 512], F32, tag="tg")
+                    nc.gpsimd.tensor_scalar(
+                        out=tg[:], in0=zc[:], scalar1=coef[:, 2:3], scalar2=coef[:, 1:2], op0=ALU.mult, op1=ALU.add
+                    )
+                    nc.gpsimd.tensor_tensor(out=tg[:], in0=tg[:], in1=zc[:], op=ALU.mult)
+                    nc.gpsimd.tensor_scalar(
+                        out=tg[:], in0=tg[:], scalar1=unit[:, 0:1], scalar2=coef[:, 0:1], op0=ALU.mult, op1=ALU.add
+                    )
+                    nc.gpsimd.tensor_tensor(out=res[:, a, :], in0=tg[:], in1=zc[:], op=ALU.mult)
+                else:
+                    t = poly_pool.tile([P, 512], F32, tag="t")
+                    nc.scalar.activation(
+                        out=t[:], in_=zs[a][:], func=ACT.Identity, bias=coef[:, 1:2], scale=coef[:, 2:3]
+                    )
+                    ts[a] = t
 
             def second(a):
                 nc.vector.tensor_tensor(out=ts[a][:], in0=ts[a][:], in1=zs[a][:], op=ALU.mult)
@@ -185,17 +205,25 @@ def tile_sketchgcn_pa_kernel(tc, nf_mats, conv_mats, W1, b1, c1, out):
                     out=res[:, a, :], in0=ts[a][:], scalar=coef[:, 0:1], in1=zs[a][:], op0=ALU.add, op1=ALU.mult
                 )
 
-            if i < 7:
+            def store(a):
+                nc.sync.dma_start(out=out_rows[:, a, :], in_=res[:, a, :])
+
+            late = []
+            if any(on_gpsimd) or i == 7:
+                for a in range(2):
+                    if on_gpsimd[a]:
+                        late.append(a)
+                    else:
+                        second(a)
+                        third(a)
+                        store(a)
+            else:
                 second(0)
                 second(1)
                 third(0)
                 third(1)
                 nc.sync.dma_start(out=out_rows, in_=res[:])
-            else:
-                for a in range(2):
-                    second(a)
-                    third(a)
-                    nc.sync.dma_start(out=out_rows[:, a, :], in_=res[:, a, :])
+            return [(store, a) for a in late]
 
         nf_g = {}
         nf_q = {}
@@ -231,8 +259,12 @@ def tile_sketchgcn_pa_kernel(tc, nf_mats, conv_mats, W1, b1, c1, out):
         for i in range(2, LOOKAHEAD):
             cv_g[i] = front_cv(i)
             cv_q[i] = quantise(cv_g[i], cvc_pool, "cv")
+        late_stores = []
         for i in range(8):
-            back_cv(i, cv_q[i])
+            later = back_cv(i, cv_q[i])
+            for store_fn, a in late_stores:
+                store_fn(a)
+            late_stores = later
             if i + LOOKAHEAD < 8:
                 cv_g[i + LOOKAHEAD] = front_cv(i + LOOKAHEAD)
                 cv_q[i + LOOKAHEAD] = quantise(cv_g[i + LOOKAHEAD], cvc_pool, "cv")

@@ -192,13 +192,13 @@ def tile_sketchgcn_pa_kernel(tc, nf_mats, conv_mats, W1, b1, c1, out):
                     nc.gpsimd.tensor_tensor(out=res[:, a, :], in0=tg[:], in1=zc[:], op=ALU.mult)
                 else:
                     t = poly_pool.tile([P, 512], F32, tag="t")
-                    nc.scalar.activation(
-                        out=t[:], in_=zs[a][:], func=ACT.Identity, bias=coef[:, 1:2], scale=coef[:, 2:3]
-                    )
+                    nc.scalar.activation(out=t[:], in_=zs[a][:], func=ACT.Identity, scale=coef[:, 2:3])
                     ts[a] = t
 
             def second(a):
-                nc.vector.tensor_tensor(out=ts[a][:], in0=ts[a][:], in1=zs[a][:], op=ALU.mult)
+                nc.vector.scalar_tensor_tensor(
+                    out=ts[a][:], in0=ts[a][:], scalar=coef[:, 1:2], in1=zs[a][:], op0=ALU.add, op1=ALU.mult
+                )
 
             def third(a):
                 nc.vector.scalar_tensor_tensor(

@@ -15,8 +15,9 @@ P = 128
 NT, N, C_IN, C_H = 2048, 2048, 1024, 512
 FLOPS = 2 * N * C_IN * C_H + 2 * NT * N * C_H
 
-LOOKAHEAD = 3
-GPSIMD_TILES = ((1, 1), (3, 1), (5, 1))
+LOOKAHEAD = 2
+GPSIMD_TILES = ((1, 1), (3, 1))
+LAST_WIDTH = 256
 
 
 def tile_sketchgcn_pa_kernel(tc, nf_mats, conv_mats, W1, b1, c1, out):
@@ -37,25 +38,30 @@ def tile_sketchgcn_pa_kernel(tc, nf_mats, conv_mats, W1, b1, c1, out):
         ps_m = ctx.enter_context(tc.psum_pool(name="ps_m", bufs=4))
         ctx.enter_context(tc.manual_schedule())
 
-        ident = const.tile([P, P], F32)
-        make_identity(nc, ident[:])
-        row = const.tile([P, C_H + 32], BF16)
-        nc.vector.memset(row[:], 0.0)
-        ones = const.tile([P, P], BF16)
-        nc.vector.memset(ones[:], 1.0)
+        busy = const.tile([P, 512], BF16)
+        nc.vector.memset(busy[:].bitcast(U32), 0)
         unit = const.tile([P, 1], F32)
         nc.vector.memset(unit[:], 1.0)
-        nc.scalar.dma_start(out=row[0:1, 0:C_H], in_=b1.rearrange("(o c) -> o c", o=1))
-        nc.scalar.dma_start(out=row[0:1, C_H : C_H + 3], in_=c1.rearrange("(o c) -> o c", o=1))
+        warm = const.tile([P, 1], F32)
+        nc.scalar.activation(out=warm[:], in_=unit[:], func=ACT.Identity)
+        ident = const.tile([P, P], F32)
+        make_identity(nc, ident[:])
+        ones = const.tile([P, P], BF16)
+        nc.vector.memset(ones[:], 1.0)
+        row = const.tile([P, C_H + 32], BF16)
+        nc.vector.memset(row[:], 0.0)
 
         w1_raw = const.tile([P, 8, C_H], BF16)
-        for half in range(2):
-            nc.sync.dma_start(
-                out=w1_raw[:, 4 * half : 4 * half + 4, :].rearrange("q (u e) c -> q u e c", u=2),
-                in_=W1[512 * half : 512 * half + 512, :].rearrange("(u q e) c -> q u e c", u=2, e=2),
-            )
         nf_raw = []
         for r in range(8):
+            if r == 2:
+                nc.sync.dma_start(out=row[0:1, 0:C_H], in_=b1.rearrange("(o c) -> o c", o=1))
+                nc.sync.dma_start(out=row[0:1, C_H : C_H + 3], in_=c1.rearrange("(o c) -> o c", o=1))
+                for half in range(2):
+                    nc.sync.dma_start(
+                        out=w1_raw[:, 4 * half : 4 * half + 4, :].rearrange("q (u e) c -> q u e c", u=2),
+                        in_=W1[512 * half : 512 * half + 512, :].rearrange("(u q e) c -> q u e c", u=2, e=2),
+                    )
             nfr = nf_pool.tile([P, 2 * C_IN], BF16, tag="nfr")
             nc.sync.dma_start(
                 out=nfr[:].rearrange("j (e k) -> j e k", e=2),
@@ -74,37 +80,40 @@ def tile_sketchgcn_pa_kernel(tc, nf_mats, conv_mats, W1, b1, c1, out):
         w1_grouped = const.tile([P, 2, C_H, 4], BF16, align_bytes=64)
         w1_codes = const.tile([P, 2 * C_H], U32, align_bytes=64)
         w1_scales = const.tile([P, 2 * C_H], U8, align_bytes=64)
-        for half in range(2):
-            nc.vector.tensor_copy(
-                out=w1_grouped[:, half, :, :].rearrange("p (c i) t -> p c t i", i=4),
-                in_=w1_raw[:, 4 * half : 4 * half + 4, :].rearrange("p t (c i) -> p c t i", i=4),
+
+        def regroup_w1(half, cols, copy):
+            copy(
+                out=w1_grouped[:, half, cols, :].rearrange("p (c i) t -> p c t i", i=4),
+                in_=w1_raw[:, 4 * half : 4 * half + 4, cols].rearrange("p t (c i) -> p c t i", i=4),
             )
-        nc.vector.quantize_mx(
-            out=w1_codes[:].bitcast(FP8X4),
-            scales=w1_scales[:],
-            in_=w1_grouped[:].rearrange("p h c t -> p (h c t)"),
-        )
+
+        def quantise_w1(half, cols):
+            words = slice(512 * half + cols.start, 512 * half + cols.stop)
+            nc.vector.quantize_mx(
+                out=w1_codes[:, words].bitcast(FP8X4),
+                scales=w1_scales[:, words],
+                in_=w1_grouped[:, half, cols, :].rearrange("p c t -> p (c t)"),
+            )
+
         bias = const.tile([P, C_H], F32)
         coef = const.tile([P, 32], F32)
 
         h_codes = const.tile([P, 4 * C_H], U32, align_bytes=64)
         h_scales = const.tile([P, 4 * C_H], U8, align_bytes=64)
 
-        def front(raw_words, grouped_pool, tag):
-            grouped = grouped_pool.tile([P, 4096], BF16, tag=tag + "g", align_bytes=64)
+        def transposes(raw_words, grouped, first):
             g32 = grouped[:].bitcast(F32)
             banks = []
-            for b in range(4):
+            for words in raw_words:
                 tp = ps_t.tile([P, 512], F32, tag="tp")
                 for s in range(4):
-                    nc.tensor.transpose(out=tp[:, 128 * s : 128 * s + 128], in_=raw_words[b][s], identity=ident[:])
+                    nc.tensor.transpose(out=tp[:, 128 * s : 128 * s + 128], in_=words[s], identity=ident[:])
                 banks.append(tp)
-            for b in range(4):
+            for b, tp in enumerate(banks, first):
                 nc.scalar.copy(
                     out=g32[:, 512 * b : 512 * b + 512].rearrange("p (a j u) -> p a j u", a=2, u=2),
-                    in_=banks[b][:].rearrange("p (a u j) -> p a j u", a=2, u=2),
+                    in_=tp[:].rearrange("p (a u j) -> p a j u", a=2, u=2),
                 )
-            return grouped
 
         def quantise(grouped, codes_pool, tag):
             codes = codes_pool.tile([P, 1024], U32, tag=tag + "c", align_bytes=64)
@@ -112,23 +121,37 @@ def tile_sketchgcn_pa_kernel(tc, nf_mats, conv_mats, W1, b1, c1, out):
             nc.vector.quantize_mx(out=codes[:].bitcast(FP8X4), scales=scales[:], in_=grouped[:])
             return codes, scales
 
-        def front_nf(g):
-            words = []
-            for ue in range(4):
-                src = nf_raw[2 * g + ue // 2][:].bitcast(F32)
-                base = 512 * (ue % 2)
-                words.append([src[:, base + 128 * s : base + 128 * s + 128] for s in range(4)])
-            return front(words, nfg_pool, "nf")
+        def nf_words(g, half):
+            src = nf_raw[2 * g + half][:].bitcast(F32)
+            return [[src[:, 512 * e + 128 * s : 512 * e + 128 * s + 128] for s in range(4)] for e in range(2)]
+
+        def front_nf(g, halves=(0, 1)):
+            if g not in nf_g:
+                grouped = nfg_pool.tile([P, 4096], BF16, tag="nfg", align_bytes=64)
+                nf_g[g] = grouped
+            for half in halves:
+                transposes(nf_words(g, half), nf_g[g], 2 * half)
 
         def front_cv(i):
             src = cv_raw[i][:].bitcast(F32)
+            grouped = cvg_pool.tile([P, 4096], BF16, tag="cvg", align_bytes=64)
             words = [[src[:, 512 * b + 128 * s : 512 * b + 128 * s + 128] for s in range(4)] for b in range(4)]
-            return front(words, cvg_pool, "cv")
+            transposes(words, grouped, 0)
+            return grouped
 
-        def back_nf(nf_q):
-            codes, scales = nf_q
-            hg = hg_pool.tile([P, 4 * C_H], BF16, tag="hg", align_bytes=64)
-            for cb in range(4):
+        def stay_warm(count):
+            idle = ps_m.tile([P, 512], F32, tag="mm")
+            for n in range(count):
+                nc.tensor.matmul(out=idle[:], lhsT=busy[:, 0:P], rhs=busy[:], start=True, stop=True)
+
+        def back_nf(g, cbs=(0, 1, 2, 3)):
+            codes, scales = nf_q[g]
+            if g not in hgs:
+                hg_new = hg_pool.tile([P, 4 * C_H], BF16, tag="hg", align_bytes=64)
+                hgs[g] = hg_new
+            hg = hgs[g]
+            accs = []
+            for cb in cbs:
                 acc = ps_m.tile([P, 512], F32, tag="mm")
                 for ue in range(4):
                     for kp in range(2):
@@ -143,44 +166,59 @@ def tile_sketchgcn_pa_kernel(tc, nf_mats, conv_mats, W1, b1, c1, out):
                             start=(kp == 0),
                             stop=(kp == 1),
                         )
-                nc.vector.tensor_tensor(
-                    out=hg[:, 512 * cb : 512 * cb + 512].rearrange("p (c t) -> p c t", t=4),
-                    in0=acc[:].rearrange("p (t c) -> p c t", t=4),
-                    in1=bias[:, 128 * cb : 128 * cb + 128].unsqueeze(2).to_broadcast([P, 128, 4]),
-                    op=ALU.add,
-                )
-            return hg
+                accs.append(acc)
+            return accs
 
-        def quant_h(g, hg):
+        def add_bias(g, cbs, accs):
+            hg = hgs[g]
+            for cb, acc in zip(cbs, accs):
+                dst = hg[:, 512 * cb : 512 * cb + 512].rearrange("p (c t) -> p c t", t=4)
+                prod = acc[:].rearrange("p (t c) -> p c t", t=4)
+                bias_c = bias[:, 128 * cb : 128 * cb + 128].unsqueeze(2).to_broadcast([P, 128, 4])
+                if cb == 0:
+                    hs = gp_pool.tile([P, 128, 4], F32, tag="hs")
+                    nc.scalar.copy(out=hs[:], in_=prod)
+                    nc.gpsimd.tensor_tensor(out=dst, in0=hs[:], in1=bias_c, op=ALU.add)
+                else:
+                    nc.vector.tensor_tensor(out=dst, in0=prod, in1=bias_c, op=ALU.add)
+
+        def quant_h(g):
+            hg = hgs[g]
             cols = slice(C_H * g, C_H * g + C_H)
             nc.vector.quantize_mx(out=h_codes[:, cols].bitcast(FP8X4), scales=h_scales[:, cols], in_=hg[:])
 
         def back_cv(i, cv_q):
             codes, scales = cv_q
-            zs = []
-            for a in range(2):
-                z = ps_m.tile([P, 512], F32, tag="mm")
-                for g in range(4):
-                    m_cols = slice(128 * (4 * a + g), 128 * (4 * a + g) + 128)
-                    n_cols = slice(C_H * g, C_H * g + C_H)
-                    nc.tensor.matmul_mx(
-                        out=z[:],
-                        lhsT=codes[:, m_cols].bitcast(FP8X4),
-                        lhsT_scale=scales[:, m_cols],
-                        rhs=h_codes[:, n_cols].bitcast(FP8X4),
-                        rhs_scale=h_scales[:, n_cols],
-                        start=(g == 0),
-                        stop=(g == 3),
-                    )
-                zs.append(z)
             res = res_pool.tile([P, 2, C_H], F32, tag="res")
             out_rows = out[256 * i : 256 * i + 256, :].rearrange("(p a) c -> p a c", a=2)
-            on_gpsimd = [(i, a) in GPSIMD_TILES for a in range(2)]
-            ts = {}
+            pieces = []
             for a in range(2):
-                if on_gpsimd[a]:
+                width = LAST_WIDTH if (i, a) == (7, 1) else C_H
+                for c0 in range(0, C_H, width):
+                    z = ps_m.tile([P, 512], F32, tag="mm")
+                    for g in range(4):
+                        m_cols = slice(128 * (4 * a + g), 128 * (4 * a + g) + 128)
+                        n_cols = slice(C_H * g + c0, C_H * g + c0 + width)
+                        nc.tensor.matmul_mx(
+                            out=z[:, 0:width],
+                            lhsT=codes[:, m_cols].bitcast(FP8X4),
+                            lhsT_scale=scales[:, m_cols],
+                            rhs=h_codes[:, n_cols].bitcast(FP8X4),
+                            rhs_scale=h_scales[:, n_cols],
+                            start=(g == 0),
+                            stop=(g == 3),
+                        )
+                    pieces.append((a, slice(c0, c0 + width), z[:, 0:width]))
+
+            first = []
+            last = []
+            late = []
+            for a, cols, z in pieces:
+                width = cols.stop - cols.start
+                dst = res[:, a, cols]
+                if (i, a) in GPSIMD_TILES:
                     zc = gp_pool.tile([P, 512], F32, tag="zc")
-                    nc.scalar.copy(out=zc[:], in_=zs[a][:])
+                    nc.scalar.copy(out=zc[:], in_=z)
                     tg = gp_pool.tile([P, 512], F32, tag="tg")
                     nc.gpsimd.tensor_scalar(
                         out=tg[:], in0=zc[:], scalar1=coef[:, 2:3], scalar2=coef[:, 1:2], op0=ALU.mult, op1=ALU.add
@@ -189,82 +227,123 @@ def tile_sketchgcn_pa_kernel(tc, nf_mats, conv_mats, W1, b1, c1, out):
                     nc.gpsimd.tensor_scalar(
                         out=tg[:], in0=tg[:], scalar1=unit[:, 0:1], scalar2=coef[:, 0:1], op0=ALU.mult, op1=ALU.add
                     )
-                    nc.gpsimd.tensor_tensor(out=res[:, a, :], in0=tg[:], in1=zc[:], op=ALU.mult)
+                    nc.gpsimd.tensor_tensor(out=dst, in0=tg[:], in1=zc[:], op=ALU.mult)
+                    late.append((a, cols))
                 else:
                     t = poly_pool.tile([P, 512], F32, tag="t")
-                    nc.scalar.activation(out=t[:], in_=zs[a][:], func=ACT.Identity, scale=coef[:, 2:3])
-                    ts[a] = t
+                    nc.scalar.activation(out=t[:, 0:width], in_=z, func=ACT.Identity, scale=coef[:, 2:3])
+                    first.append((t[:, 0:width], z))
+                    last.append((a, cols, (dst, t[:, 0:width], z)))
 
-            def second(a):
-                nc.vector.scalar_tensor_tensor(
-                    out=ts[a][:], in0=ts[a][:], scalar=coef[:, 1:2], in1=zs[a][:], op0=ALU.add, op1=ALU.mult
-                )
+            def store(a, cols):
+                nc.sync.dma_start(out=out_rows[:, a, cols], in_=res[:, a, cols])
 
-            def third(a):
-                nc.vector.scalar_tensor_tensor(
-                    out=res[:, a, :], in0=ts[a][:], scalar=coef[:, 0:1], in1=zs[a][:], op0=ALU.add, op1=ALU.mult
-                )
+            def second(t, z):
+                nc.vector.scalar_tensor_tensor(out=t, in0=t, scalar=coef[:, 1:2], in1=z, op0=ALU.add, op1=ALU.mult)
 
-            def store(a):
-                nc.sync.dma_start(out=out_rows[:, a, :], in_=res[:, a, :])
+            def third(dst, t, z):
+                nc.vector.scalar_tensor_tensor(out=dst, in0=t, scalar=coef[:, 0:1], in1=z, op0=ALU.add, op1=ALU.mult)
 
-            late = []
-            if any(on_gpsimd) or i == 7:
-                for a in range(2):
-                    if on_gpsimd[a]:
-                        late.append(a)
-                    else:
-                        second(a)
-                        third(a)
-                        store(a)
+            if i == 7:
+                second(*first[0])
+                second(*first[1])
+                third(*last[0][2])
+                store(*last[0][:2])
+                third(*last[1][2])
+                store(*last[1][:2])
+                second(*first[2])
+                third(*last[2][2])
+                store(*last[2][:2])
             else:
-                second(0)
-                second(1)
-                third(0)
-                third(1)
-                nc.sync.dma_start(out=out_rows, in_=res[:])
-            return [(store, a) for a in late]
+                for t, z in first:
+                    second(t, z)
+                for a, cols, args in last:
+                    third(*args)
+                if len(last) == 2:
+                    nc.sync.dma_start(out=out_rows, in_=res[:])
+                else:
+                    for a, cols, args in last:
+                        store(a, cols)
+
+            def finish():
+                for a, cols in late:
+                    store(a, cols)
+
+            return finish
 
         nf_g = {}
         nf_q = {}
         cv_g = {}
         cv_q = {}
         hgs = {}
-        nf_g[0] = front_nf(0)
-        nf_q[0] = quantise(nf_g[0], nfc_pool, "nf")
-        nf_g[1] = front_nf(1)
+        ALL = (0, 1, 2, 3)
+        stay_warm(4)
+        front_nf(0, (0,))
+        stay_warm(1)
+        front_nf(0, (1,))
         bias_ps = ps_m.tile([P, 512], F32, tag="mm")
         nc.tensor.matmul(out=bias_ps[:], lhsT=ones[:], rhs=row[:, 0:C_H], start=True, stop=True)
         coef_ps = ps_m.tile([P, 512], F32, tag="mm")
         nc.tensor.matmul(out=coef_ps[:, 0:32], lhsT=ones[:], rhs=row[:, C_H : C_H + 32], start=True, stop=True)
-        nc.vector.tensor_copy(out=bias[:], in_=bias_ps[:])
-        nc.vector.tensor_copy(out=coef[:], in_=coef_ps[:, 0:32])
-        hgs[0] = back_nf(nf_q[0])
+        stay_warm(4)
+        codes0 = nfc_pool.tile([P, 1024], U32, tag="nfc", align_bytes=64)
+        scales0 = nfc_pool.tile([P, 1024], U8, tag="nfs", align_bytes=64)
+        nf_q[0] = (codes0, scales0)
+
+        def quantise_nf0(half):
+            cols = slice(512 * half, 512 * half + 512)
+            nc.vector.quantize_mx(
+                out=codes0[:, cols].bitcast(FP8X4),
+                scales=scales0[:, cols],
+                in_=nf_g[0][:, 2048 * half : 2048 * half + 2048],
+            )
+
+        left = slice(0, 256)
+        right = slice(256, 512)
+        quantise_nf0(0)
+        regroup_w1(0, left, nc.vector.tensor_copy)
+        regroup_w1(0, right, nc.scalar.copy)
+        nc.scalar.copy(out=bias[:], in_=bias_ps[:])
+        nc.scalar.copy(out=coef[:], in_=coef_ps[:, 0:32])
+        quantise_w1(0, left)
+        regroup_w1(1, slice(0, 128), nc.vector.tensor_copy)
+        quantise_nf0(1)
+        quantise_w1(1, slice(0, 128))
+        regroup_w1(1, slice(128, 256), nc.vector.tensor_copy)
+        quantise_w1(1, slice(128, 256))
+        regroup_w1(1, right, nc.vector.tensor_copy)
+        quantise_w1(0, right)
+        quantise_w1(1, right)
+        add_bias(0, (0, 1), back_nf(0, (0, 1)))
+        front_nf(1)
+        accs = back_nf(0, (2, 3))
         nf_q[1] = quantise(nf_g[1], nfc_pool, "nf")
-        quant_h(0, hgs[0])
-        nf_g[2] = front_nf(2)
+        add_bias(0, (2, 3), accs)
+        front_nf(2)
+        accs = back_nf(1)
+        quant_h(0)
         nf_q[2] = quantise(nf_g[2], nfc_pool, "nf")
-        nf_g[3] = front_nf(3)
-        hgs[1] = back_nf(nf_q[1])
+        add_bias(1, ALL, accs)
+        front_nf(3)
+        accs = back_nf(2)
+        quant_h(1)
         nf_q[3] = quantise(nf_g[3], nfc_pool, "nf")
-        quant_h(1, hgs[1])
+        add_bias(2, ALL, accs)
         cv_g[0] = front_cv(0)
-        hgs[2] = back_nf(nf_q[2])
+        accs = back_nf(3)
+        quant_h(2)
+        add_bias(3, (0, 1), accs[:2])
         cv_q[0] = quantise(cv_g[0], cvc_pool, "cv")
+        add_bias(3, (2, 3), accs[2:])
         cv_g[1] = front_cv(1)
-        hgs[3] = back_nf(nf_q[3])
-        quant_h(2, hgs[2])
-        quant_h(3, hgs[3])
+        quant_h(3)
         cv_q[1] = quantise(cv_g[1], cvc_pool, "cv")
-        for i in range(2, LOOKAHEAD):
-            cv_g[i] = front_cv(i)
-            cv_q[i] = quantise(cv_g[i], cvc_pool, "cv")
-        late_stores = []
+        finish = None
         for i in range(8):
-            later = back_cv(i, cv_q[i])
-            for store_fn, a in late_stores:
-                store_fn(a)
-            late_stores = later
+            finish_next = back_cv(i, cv_q[i])
+            if finish is not None:
+                finish()
+            finish = finish_next
             if i + LOOKAHEAD < 8:
                 cv_g[i + LOOKAHEAD] = front_cv(i + LOOKAHEAD)
                 cv_q[i + LOOKAHEAD] = quantise(cv_g[i + LOOKAHEAD], cvc_pool, "cv")

@@ -15,8 +15,9 @@ P = 128
 NT, N, C_IN, C_H = 2048, 2048, 1024, 512
 FLOPS = 2 * N * C_IN * C_H + 2 * NT * N * C_H
 
-LOOKAHEAD = 2
-GPSIMD_TILES = ((1, 1), (3, 1))
+LOOKAHEAD = 3
+GPSIMD_TILES = ((1, 1), (3, 1), (5, 0))
+GPSIMD_ADDS = tuple((g, 0) for g in range(4))
 LAST_WIDTH = 256
 
 
@@ -57,6 +58,7 @@ def tile_sketchgcn_pa_kernel(tc, nf_mats, conv_mats, W1, b1, c1, out):
             if r == 2:
                 nc.sync.dma_start(out=row[0:1, 0:C_H], in_=b1.rearrange("(o c) -> o c", o=1))
                 nc.sync.dma_start(out=row[0:1, C_H : C_H + 3], in_=c1.rearrange("(o c) -> o c", o=1))
+            if r == 1:
                 for half in range(2):
                     nc.sync.dma_start(
                         out=w1_raw[:, 4 * half : 4 * half + 4, :].rearrange("q (u e) c -> q u e c", u=2),
@@ -144,16 +146,20 @@ def tile_sketchgcn_pa_kernel(tc, nf_mats, conv_mats, W1, b1, c1, out):
             for n in range(count):
                 nc.tensor.matmul(out=idle[:], lhsT=busy[:, 0:P], rhs=busy[:], start=True, stop=True)
 
-        def back_nf(g, cbs=(0, 1, 2, 3)):
-            codes, scales = nf_q[g]
-            if g not in hgs:
-                hg_new = hg_pool.tile([P, 4 * C_H], BF16, tag="hg", align_bytes=64)
-                hgs[g] = hg_new
-            hg = hgs[g]
+        def open_nf(g):
+            hg = hg_pool.tile([P, 4 * C_H], BF16, tag="hg", align_bytes=64)
+            hgs[g] = hg
             accs = []
-            for cb in cbs:
+            for cb in range(4):
                 acc = ps_m.tile([P, 512], F32, tag="mm")
-                for ue in range(4):
+                accs.append(acc)
+            return accs
+
+        def back_nf(g, accs, cbs=(0, 1, 2, 3), ues=(0, 1, 2, 3)):
+            codes, scales = nf_q[g]
+            for cb in cbs:
+                acc = accs[cb]
+                for ue in ues:
                     for kp in range(2):
                         m_cols = slice(128 * (2 * ue + kp), 128 * (2 * ue + kp) + 128)
                         n_cols = slice(512 * kp + 128 * cb, 512 * kp + 128 * cb + 128)
@@ -166,16 +172,15 @@ def tile_sketchgcn_pa_kernel(tc, nf_mats, conv_mats, W1, b1, c1, out):
                             start=(kp == 0),
                             stop=(kp == 1),
                         )
-                accs.append(acc)
-            return accs
 
-        def add_bias(g, cbs, accs):
+        def add_bias(g, accs, cbs=(0, 1, 2, 3)):
             hg = hgs[g]
-            for cb, acc in zip(cbs, accs):
+            for cb in cbs:
+                acc = accs[cb]
                 dst = hg[:, 512 * cb : 512 * cb + 512].rearrange("p (c t) -> p c t", t=4)
                 prod = acc[:].rearrange("p (t c) -> p c t", t=4)
                 bias_c = bias[:, 128 * cb : 128 * cb + 128].unsqueeze(2).to_broadcast([P, 128, 4])
-                if cb == 0:
+                if (g, cb) in GPSIMD_ADDS:
                     hs = gp_pool.tile([P, 128, 4], F32, tag="hs")
                     nc.scalar.copy(out=hs[:], in_=prod)
                     nc.gpsimd.tensor_tensor(out=dst, in0=hs[:], in1=bias_c, op=ALU.add)
@@ -187,29 +192,34 @@ def tile_sketchgcn_pa_kernel(tc, nf_mats, conv_mats, W1, b1, c1, out):
             cols = slice(C_H * g, C_H * g + C_H)
             nc.vector.quantize_mx(out=h_codes[:, cols].bitcast(FP8X4), scales=h_scales[:, cols], in_=hg[:])
 
-        def back_cv(i, cv_q):
-            codes, scales = cv_q
-            res = res_pool.tile([P, 2, C_H], F32, tag="res")
-            out_rows = out[256 * i : 256 * i + 256, :].rearrange("(p a) c -> p a c", a=2)
+        def open_cv(i):
             pieces = []
             for a in range(2):
                 width = LAST_WIDTH if (i, a) == (7, 1) else C_H
                 for c0 in range(0, C_H, width):
                     z = ps_m.tile([P, 512], F32, tag="mm")
-                    for g in range(4):
-                        m_cols = slice(128 * (4 * a + g), 128 * (4 * a + g) + 128)
-                        n_cols = slice(C_H * g + c0, C_H * g + c0 + width)
-                        nc.tensor.matmul_mx(
-                            out=z[:, 0:width],
-                            lhsT=codes[:, m_cols].bitcast(FP8X4),
-                            lhsT_scale=scales[:, m_cols],
-                            rhs=h_codes[:, n_cols].bitcast(FP8X4),
-                            rhs_scale=h_scales[:, n_cols],
-                            start=(g == 0),
-                            stop=(g == 3),
-                        )
                     pieces.append((a, slice(c0, c0 + width), z[:, 0:width]))
+            return pieces
 
+        def back_cv(i, pieces, gs=(0, 1, 2, 3)):
+            codes, scales = cv_q[i]
+            for a, cols, z in pieces:
+                for g in gs:
+                    m_cols = slice(128 * (4 * a + g), 128 * (4 * a + g) + 128)
+                    n_cols = slice(C_H * g + cols.start, C_H * g + cols.stop)
+                    nc.tensor.matmul_mx(
+                        out=z,
+                        lhsT=codes[:, m_cols].bitcast(FP8X4),
+                        lhsT_scale=scales[:, m_cols],
+                        rhs=h_codes[:, n_cols].bitcast(FP8X4),
+                        rhs_scale=h_scales[:, n_cols],
+                        start=(g == 0),
+                        stop=(g == 3),
+                    )
+
+        def polynomial(i, pieces):
+            res = res_pool.tile([P, 2, C_H], F32, tag="res")
+            out_rows = out[256 * i : 256 * i + 256, :].rearrange("(p a) c -> p a c", a=2)
             first = []
             last = []
             late = []
@@ -279,13 +289,7 @@ def tile_sketchgcn_pa_kernel(tc, nf_mats, conv_mats, W1, b1, c1, out):
         ALL = (0, 1, 2, 3)
         stay_warm(4)
         front_nf(0, (0,))
-        stay_warm(1)
-        front_nf(0, (1,))
-        bias_ps = ps_m.tile([P, 512], F32, tag="mm")
-        nc.tensor.matmul(out=bias_ps[:], lhsT=ones[:], rhs=row[:, 0:C_H], start=True, stop=True)
-        coef_ps = ps_m.tile([P, 512], F32, tag="mm")
-        nc.tensor.matmul(out=coef_ps[:, 0:32], lhsT=ones[:], rhs=row[:, C_H : C_H + 32], start=True, stop=True)
-        stay_warm(4)
+        stay_warm(5)
         codes0 = nfc_pool.tile([P, 1024], U32, tag="nfc", align_bytes=64)
         scales0 = nfc_pool.tile([P, 1024], U8, tag="nfs", align_bytes=64)
         nf_q[0] = (codes0, scales0)
@@ -300,47 +304,60 @@ def tile_sketchgcn_pa_kernel(tc, nf_mats, conv_mats, W1, b1, c1, out):
 
         left = slice(0, 256)
         right = slice(256, 512)
-        quantise_nf0(0)
         regroup_w1(0, left, nc.vector.tensor_copy)
         regroup_w1(0, right, nc.scalar.copy)
+        quantise_nf0(0)
+        regroup_w1(1, left, nc.vector.tensor_copy)
+        regroup_w1(1, right, nc.scalar.copy)
+        quantise_w1(0, left)
+        quantise_w1(1, left)
+        front_nf(0, (1,))
+        bias_ps = ps_t.tile([P, 512], F32, tag="tp")
+        coef_ps = ps_t.tile([P, 512], F32, tag="tp")
+        nc.tensor.matmul(out=bias_ps[:], lhsT=ones[:], rhs=row[:, 0:C_H], start=True, stop=True)
+        nc.tensor.matmul(out=coef_ps[:, 0:32], lhsT=ones[:], rhs=row[:, C_H : C_H + 32], start=True, stop=True)
         nc.scalar.copy(out=bias[:], in_=bias_ps[:])
         nc.scalar.copy(out=coef[:], in_=coef_ps[:, 0:32])
-        quantise_w1(0, left)
-        regroup_w1(1, slice(0, 128), nc.vector.tensor_copy)
-        quantise_nf0(1)
-        quantise_w1(1, slice(0, 128))
-        regroup_w1(1, slice(128, 256), nc.vector.tensor_copy)
-        quantise_w1(1, slice(128, 256))
-        regroup_w1(1, right, nc.vector.tensor_copy)
         quantise_w1(0, right)
         quantise_w1(1, right)
-        add_bias(0, (0, 1), back_nf(0, (0, 1)))
+        accs = open_nf(0)
+        back_nf(0, accs, ues=(0, 1))
+        quantise_nf0(1)
         front_nf(1)
-        accs = back_nf(0, (2, 3))
+        back_nf(0, accs, ues=(2, 3))
+        add_bias(0, accs, (0, 1))
         nf_q[1] = quantise(nf_g[1], nfc_pool, "nf")
-        add_bias(0, (2, 3), accs)
-        front_nf(2)
-        accs = back_nf(1)
-        quant_h(0)
-        nf_q[2] = quantise(nf_g[2], nfc_pool, "nf")
-        add_bias(1, ALL, accs)
-        front_nf(3)
-        accs = back_nf(2)
-        quant_h(1)
-        nf_q[3] = quantise(nf_g[3], nfc_pool, "nf")
-        add_bias(2, ALL, accs)
-        cv_g[0] = front_cv(0)
-        accs = back_nf(3)
-        quant_h(2)
-        add_bias(3, (0, 1), accs[:2])
-        cv_q[0] = quantise(cv_g[0], cvc_pool, "cv")
-        add_bias(3, (2, 3), accs[2:])
+        add_bias(0, accs, (2, 3))
+        for g in (1, 2, 3):
+            if g < 3:
+                front_nf(g + 1)
+            else:
+                cv_g[0] = front_cv(0)
+            accs = open_nf(g)
+            back_nf(g, accs)
+            quant_h(g - 1)
+            if g < 3:
+                nf_q[g + 1] = quantise(nf_g[g + 1], nfc_pool, "nf")
+                add_bias(g, accs)
+            else:
+                add_bias(g, accs, (0, 1))
+                cv_q[0] = quantise(cv_g[0], cvc_pool, "cv")
+                add_bias(g, accs, (2, 3))
         cv_g[1] = front_cv(1)
         quant_h(3)
         cv_q[1] = quantise(cv_g[1], cvc_pool, "cv")
         finish = None
         for i in range(8):
-            finish_next = back_cv(i, cv_q[i])
+            pieces = open_cv(i)
+            if i == 0:
+                back_cv(i, pieces, (0, 1, 2))
+                cv_g[2] = front_cv(2)
+                back_cv(i, pieces, (3,))
+            else:
+                back_cv(i, pieces)
+            finish_next = polynomial(i, pieces)
+            if i == 0:
+                cv_q[2] = quantise(cv_g[2], cvc_pool, "cv")
             if finish is not None:
                 finish()
             finish = finish_next

@@ -32,7 +32,7 @@ def tile_sketchgcn_pa_kernel(tc, nf_mats, conv_mats, W1, b1, c1, out):
         hg_pool = ctx.enter_context(tc.tile_pool(name="h_grouped", bufs=2))
         cvg_pool = ctx.enter_context(tc.tile_pool(name="cv_grouped", bufs=3))
         cvc_pool = ctx.enter_context(tc.tile_pool(name="cv_codes", bufs=4))
-        poly_pool = ctx.enter_context(tc.tile_pool(name="poly", bufs=4))
+        poly_pool = ctx.enter_context(tc.tile_pool(name="poly", bufs=6))
         gp_pool = ctx.enter_context(tc.tile_pool(name="gp", bufs=2))
         res_pool = ctx.enter_context(tc.tile_pool(name="res", bufs=4))
         ps_t = ctx.enter_context(tc.psum_pool(name="ps_t", bufs=4))
@@ -103,7 +103,7 @@ def tile_sketchgcn_pa_kernel(tc, nf_mats, conv_mats, W1, b1, c1, out):
         h_codes = const.tile([P, 4 * C_H], U32, align_bytes=64)
         h_scales = const.tile([P, 4 * C_H], U8, align_bytes=64)
 
-        def transposes(raw_words, grouped, first):
+        def transposes(raw_words, grouped, first, on_vector=()):
             g32 = grouped[:].bitcast(F32)
             banks = []
             for words in raw_words:
@@ -112,7 +112,8 @@ def tile_sketchgcn_pa_kernel(tc, nf_mats, conv_mats, W1, b1, c1, out):
                     nc.tensor.transpose(out=tp[:, 128 * s : 128 * s + 128], in_=words[s], identity=ident[:])
                 banks.append(tp)
             for b, tp in enumerate(banks, first):
-                nc.scalar.copy(
+                copy = nc.vector.tensor_copy if b in on_vector else nc.scalar.copy
+                copy(
                     out=g32[:, 512 * b : 512 * b + 512].rearrange("p (a j u) -> p a j u", a=2, u=2),
                     in_=tp[:].rearrange("p (a u j) -> p a j u", a=2, u=2),
                 )
@@ -127,18 +128,18 @@ def tile_sketchgcn_pa_kernel(tc, nf_mats, conv_mats, W1, b1, c1, out):
             src = nf_raw[2 * g + half][:].bitcast(F32)
             return [[src[:, 512 * e + 128 * s : 512 * e + 128 * s + 128] for s in range(4)] for e in range(2)]
 
-        def front_nf(g, halves=(0, 1)):
+        def front_nf(g, halves=(0, 1), on_vector=()):
             if g not in nf_g:
                 grouped = nfg_pool.tile([P, 4096], BF16, tag="nfg", align_bytes=64)
                 nf_g[g] = grouped
             for half in halves:
-                transposes(nf_words(g, half), nf_g[g], 2 * half)
+                transposes(nf_words(g, half), nf_g[g], 2 * half, on_vector)
 
-        def front_cv(i):
+        def front_cv(i, on_vector=()):
             src = cv_raw[i][:].bitcast(F32)
             grouped = cvg_pool.tile([P, 4096], BF16, tag="cvg", align_bytes=64)
             words = [[src[:, 512 * b + 128 * s : 512 * b + 128 * s + 128] for s in range(4)] for b in range(4)]
-            transposes(words, grouped, 0)
+            transposes(words, grouped, 0, on_vector)
             return grouped
 
         def stay_warm(count):
@@ -197,7 +198,10 @@ def tile_sketchgcn_pa_kernel(tc, nf_mats, conv_mats, W1, b1, c1, out):
             for a in range(2):
                 width = LAST_WIDTH if (i, a) == (7, 1) else C_H
                 for c0 in range(0, C_H, width):
-                    z = ps_m.tile([P, 512], F32, tag="mm")
+                    if i == 7:
+                        z = ps_t.tile([P, 512], F32, tag="tp")
+                    else:
+                        z = ps_m.tile([P, 512], F32, tag="mm")
                     pieces.append((a, slice(c0, c0 + width), z[:, 0:width]))
             return pieces
 
@@ -239,6 +243,13 @@ def tile_sketchgcn_pa_kernel(tc, nf_mats, conv_mats, W1, b1, c1, out):
                     )
                     nc.gpsimd.tensor_tensor(out=dst, in0=tg[:], in1=zc[:], op=ALU.mult)
                     late.append((a, cols))
+                elif (i, a) == (7, 0):
+                    sq = poly_pool.tile([P, 512], F32, tag="sq", bufs=1)
+                    nc.scalar.activation(out=sq[:], in_=z, func=ACT.Square)
+                    t = poly_pool.tile([P, 512], F32, tag="t")
+                    nc.scalar.activation(out=t[:], in_=z, func=ACT.Identity, scale=coef[:, 2:3], bias=coef[:, 1:2])
+                    nc.gpsimd.tensor_tensor(out=t[:], in0=t[:], in1=sq[:], op=ALU.mult)
+                    shared = (a, cols, (dst, z, t))
                 else:
                     t = poly_pool.tile([P, 512], F32, tag="t")
                     nc.scalar.activation(out=t[:, 0:width], in_=z, func=ACT.Identity, scale=coef[:, 2:3])
@@ -259,11 +270,11 @@ def tile_sketchgcn_pa_kernel(tc, nf_mats, conv_mats, W1, b1, c1, out):
                 second(*first[1])
                 third(*last[0][2])
                 store(*last[0][:2])
+                a, cols, (dst, z, t) = shared
+                nc.vector.scalar_tensor_tensor(out=dst, in0=z, scalar=coef[:, 0:1], in1=t, op0=ALU.mult, op1=ALU.add)
+                store(a, cols)
                 third(*last[1][2])
                 store(*last[1][:2])
-                second(*first[2])
-                third(*last[2][2])
-                store(*last[2][:2])
             else:
                 for t, z in first:
                     second(t, z)
@@ -351,7 +362,7 @@ def tile_sketchgcn_pa_kernel(tc, nf_mats, conv_mats, W1, b1, c1, out):
             pieces = open_cv(i)
             if i == 0:
                 back_cv(i, pieces, (0, 1, 2))
-                cv_g[2] = front_cv(2)
+                cv_g[2] = front_cv(2, (2, 3))
                 back_cv(i, pieces, (3,))
             else:
                 back_cv(i, pieces)

@@ -17,7 +17,7 @@ FLOPS = 2 * N * C_IN * C_H + 2 * NT * N * C_H
 
 LOOKAHEAD = 3
 GPSIMD_TILES = ((1, 1), (3, 1), (5, 0))
-GPSIMD_ADDS = tuple((g, 0) for g in range(4))
+GPSIMD_ADDS = tuple((g, 1) for g in range(3))
 LAST_WIDTH = 256
 
 

@@ -55,15 +55,14 @@ def tile_sketchgcn_pa_kernel(tc, nf_mats, conv_mats, W1, b1, c1, out):
         w1_raw = const.tile([P, 8, C_H], BF16)
         nf_raw = []
         for r in range(8):
-            if r == 2:
-                nc.sync.dma_start(out=row[0:1, 0:C_H], in_=b1.rearrange("(o c) -> o c", o=1))
-                nc.sync.dma_start(out=row[0:1, C_H : C_H + 3], in_=c1.rearrange("(o c) -> o c", o=1))
             if r == 1:
                 for half in range(2):
                     nc.sync.dma_start(
                         out=w1_raw[:, 4 * half : 4 * half + 4, :].rearrange("q (u e) c -> q u e c", u=2),
                         in_=W1[512 * half : 512 * half + 512, :].rearrange("(u q e) c -> q u e c", u=2, e=2),
                     )
+                nc.sync.dma_start(out=row[0:1, 0:C_H], in_=b1.rearrange("(o c) -> o c", o=1))
+                nc.sync.dma_start(out=row[0:1, C_H : C_H + 3], in_=c1.rearrange("(o c) -> o c", o=1))
             nfr = nf_pool.tile([P, 2 * C_IN], BF16, tag="nfr")
             nc.sync.dma_start(
                 out=nfr[:].rearrange("j (e k) -> j e k", e=2),
@@ -301,6 +300,10 @@ def tile_sketchgcn_pa_kernel(tc, nf_mats, conv_mats, W1, b1, c1, out):
         stay_warm(4)
         front_nf(0, (0,))
         stay_warm(5)
+        bias_ps = ps_t.tile([P, 512], F32, tag="tp")
+        coef_ps = ps_t.tile([P, 512], F32, tag="tp")
+        nc.tensor.matmul(out=bias_ps[:], lhsT=ones[:], rhs=row[:, 0:C_H], start=True, stop=True)
+        nc.tensor.matmul(out=coef_ps[:, 0:32], lhsT=ones[:], rhs=row[:, C_H : C_H + 32], start=True, stop=True)
         codes0 = nfc_pool.tile([P, 1024], U32, tag="nfc", align_bytes=64)
         scales0 = nfc_pool.tile([P, 1024], U8, tag="nfs", align_bytes=64)
         nf_q[0] = (codes0, scales0)
@@ -322,13 +325,9 @@ def tile_sketchgcn_pa_kernel(tc, nf_mats, conv_mats, W1, b1, c1, out):
         regroup_w1(1, right, nc.scalar.copy)
         quantise_w1(0, left)
         quantise_w1(1, left)
-        front_nf(0, (1,))
-        bias_ps = ps_t.tile([P, 512], F32, tag="tp")
-        coef_ps = ps_t.tile([P, 512], F32, tag="tp")
-        nc.tensor.matmul(out=bias_ps[:], lhsT=ones[:], rhs=row[:, 0:C_H], start=True, stop=True)
-        nc.tensor.matmul(out=coef_ps[:, 0:32], lhsT=ones[:], rhs=row[:, C_H : C_H + 32], start=True, stop=True)
         nc.scalar.copy(out=bias[:], in_=bias_ps[:])
         nc.scalar.copy(out=coef[:], in_=coef_ps[:, 0:32])
+        front_nf(0, (1,))
         quantise_w1(0, right)
         quantise_w1(1, right)
         accs = open_nf(0)
@@ -351,9 +350,8 @@ def tile_sketchgcn_pa_kernel(tc, nf_mats, conv_mats, W1, b1, c1, out):
                 nf_q[g + 1] = quantise(nf_g[g + 1], nfc_pool, "nf")
                 add_bias(g, accs)
             else:
-                add_bias(g, accs, (0, 1))
                 cv_q[0] = quantise(cv_g[0], cvc_pool, "cv")
-                add_bias(g, accs, (2, 3))
+                add_bias(g, accs)
         cv_g[1] = front_cv(1)
         quant_h(3)
         cv_q[1] = quantise(cv_g[1], cvc_pool, "cv")
@@ -362,7 +360,7 @@ def tile_sketchgcn_pa_kernel(tc, nf_mats, conv_mats, W1, b1, c1, out):
             pieces = open_cv(i)
             if i == 0:
                 back_cv(i, pieces, (0, 1, 2))
-                cv_g[2] = front_cv(2, (2, 3))
+                cv_g[2] = front_cv(2, (3,))
                 back_cv(i, pieces, (3,))
             else:
                 back_cv(i, pieces)

@@ -16,7 +16,7 @@ NT, N, C_IN, C_H = 2048, 2048, 1024, 512
 FLOPS = 2 * N * C_IN * C_H + 2 * NT * N * C_H
 
 LOOKAHEAD = 3
-GPSIMD_TILES = ((1, 1), (3, 1), (5, 0))
+GPSIMD_TILES = ((5, 0),)
 GPSIMD_ADDS = tuple((g, 1) for g in range(3))
 LAST_WIDTH = 256
 
@@ -350,8 +350,9 @@ def tile_sketchgcn_pa_kernel(tc, nf_mats, conv_mats, W1, b1, c1, out):
                 nf_q[g + 1] = quantise(nf_g[g + 1], nfc_pool, "nf")
                 add_bias(g, accs)
             else:
+                add_bias(g, accs, (0,))
                 cv_q[0] = quantise(cv_g[0], cvc_pool, "cv")
-                add_bias(g, accs)
+                add_bias(g, accs, (1, 2, 3))
         cv_g[1] = front_cv(1)
         quant_h(3)
         cv_q[1] = quantise(cv_g[1], cvc_pool, "cv")

from contextlib import ExitStack

import concourse.mybir as mybir
from concourse.masks import make_identity

F32 = mybir.dt.float32
BF16 = mybir.dt.bfloat16
U32 = mybir.dt.uint32
U8 = mybir.dt.uint8
FP8X4 = mybir.dt.float8_e4m3fn_x4
ALU = mybir.AluOpType
ACT = mybir.ActivationFunctionType

P = 128
NT, N, C_IN, C_H = 2048, 2048, 1024, 512
FLOPS = 2 * N * C_IN * C_H + 2 * NT * N * C_H

LOOKAHEAD = 3
GPSIMD_TILES = ((5, 0),)
GPSIMD_ADDS = tuple((g, 1) for g in range(3))
LAST_WIDTH = 256


def tile_sketchgcn_pa_kernel(tc, nf_mats, conv_mats, W1, b1, c1, out):
    nc = tc.nc
    with ExitStack() as ctx:
        const = ctx.enter_context(tc.tile_pool(name="const", bufs=1))
        nf_pool = ctx.enter_context(tc.tile_pool(name="nf_raw", bufs=8))
        cv_pool = ctx.enter_context(tc.tile_pool(name="cv_raw", bufs=6))
        nfg_pool = ctx.enter_context(tc.tile_pool(name="nf_grouped", bufs=2))
        nfc_pool = ctx.enter_context(tc.tile_pool(name="nf_codes", bufs=2))
        hg_pool = ctx.enter_context(tc.tile_pool(name="h_grouped", bufs=2))
        cvg_pool = ctx.enter_context(tc.tile_pool(name="cv_grouped", bufs=3))
        cvc_pool = ctx.enter_context(tc.tile_pool(name="cv_codes", bufs=4))
        poly_pool = ctx.enter_context(tc.tile_pool(name="poly", bufs=6))
        gp_pool = ctx.enter_context(tc.tile_pool(name="gp", bufs=2))
        res_pool = ctx.enter_context(tc.tile_pool(name="res", bufs=4))
        ps_t = ctx.enter_context(tc.psum_pool(name="ps_t", bufs=4))
        ps_m = ctx.enter_context(tc.psum_pool(name="ps_m", bufs=4))
        ctx.enter_context(tc.manual_schedule())

        busy = const.tile([P, 512], BF16)
        nc.vector.memset(busy[:].bitcast(U32), 0)
        unit = const.tile([P, 1], F32)
        nc.vector.memset(unit[:], 1.0)
        warm = const.tile([P, 1], F32)
        nc.scalar.activation(out=warm[:], in_=unit[:], func=ACT.Identity)
        ident = const.tile([P, P], F32)
        make_identity(nc, ident[:])
        ones = const.tile([P, P], BF16)
        nc.vector.memset(ones[:], 1.0)
        row = const.tile([P, C_H + 32], BF16)
        nc.vector.memset(row[:], 0.0)

        w1_raw = const.tile([P, 8, C_H], BF16)
        nf_raw = []
        for r in range(8):
            if r == 1:
                for half in range(2):
                    nc.sync.dma_start(
                        out=w1_raw[:, 4 * half : 4 * half + 4, :].rearrange("q (u e) c -> q u e c", u=2),
                        in_=W1[512 * half : 512 * half + 512, :].rearrange("(u q e) c -> q u e c", u=2, e=2),
                    )
                nc.sync.dma_start(out=row[0:1, 0:C_H], in_=b1.rearrange("(o c) -> o c", o=1))
                nc.sync.dma_start(out=row[0:1, C_H : C_H + 3], in_=c1.rearrange("(o c) -> o c", o=1))
            nfr = nf_pool.tile([P, 2 * C_IN], BF16, tag="nfr")
            nc.sync.dma_start(
                out=nfr[:].rearrange("j (e k) -> j e k", e=2),
                in_=nf_mats[256 * r : 256 * r + 256, :].rearrange("(j e) k -> j e k", e=2),
            )
            nf_raw.append(nfr)
        cv_raw = []
        for i in range(8):
            cvr = cv_pool.tile([P, 2 * N], BF16, tag="cvr")
            nc.sync.dma_start(
                out=cvr[:].rearrange("p (a n) -> p a n", a=2),
                in_=conv_mats[256 * i : 256 * i + 256, :].rearrange("(p a) n -> p a n", a=2),
            )
            cv_raw.append(cvr)

        w1_grouped = const.tile([P, 2, C_H, 4], BF16, align_bytes=64)
        w1_codes = const.tile([P, 2 * C_H], U32, align_bytes=64)
        w1_scales = const.tile([P, 2 * C_H], U8, align_bytes=64)

        def regroup_w1(half, cols, copy):
            copy(
                out=w1_grouped[:, half, cols, :].rearrange("p (c i) t -> p c t i", i=4),
                in_=w1_raw[:, 4 * half : 4 * half + 4, cols].rearrange("p t (c i) -> p c t i", i=4),
            )

        def quantise_w1(half, cols):
            words = slice(512 * half + cols.start, 512 * half + cols.stop)
            nc.vector.quantize_mx(
                out=w1_codes[:, words].bitcast(FP8X4),
                scales=w1_scales[:, words],
                in_=w1_grouped[:, half, cols, :].rearrange("p c t -> p (c t)"),
            )

        bias = const.tile([P, C_H], F32)
        coef = const.tile([P, 32], F32)

        h_codes = const.tile([P, 4 * C_H], U32, align_bytes=64)
        h_scales = const.tile([P, 4 * C_H], U8, align_bytes=64)

        def transposes(raw_words, grouped, first, on_vector=()):
            g32 = grouped[:].bitcast(F32)
            banks = []
            for words in raw_words:
                tp = ps_t.tile([P, 512], F32, tag="tp")
                for s in range(4):
                    nc.tensor.transpose(out=tp[:, 128 * s : 128 * s + 128], in_=words[s], identity=ident[:])
                banks.append(tp)
            for b, tp in enumerate(banks, first):
                copy = nc.vector.tensor_copy if b in on_vector else nc.scalar.copy
                copy(
                    out=g32[:, 512 * b : 512 * b + 512].rearrange("p (a j u) -> p a j u", a=2, u=2),
                    in_=tp[:].rearrange("p (a u j) -> p a j u", a=2, u=2),
                )

        def quantise(grouped, codes_pool, tag):
            codes = codes_pool.tile([P, 1024], U32, tag=tag + "c", align_bytes=64)
            scales = codes_pool.tile([P, 1024], U8, tag=tag + "s", align_bytes=64)
            nc.vector.quantize_mx(out=codes[:].bitcast(FP8X4), scales=scales[:], in_=grouped[:])
            return codes, scales

        def nf_words(g, half):
            src = nf_raw[2 * g + half][:].bitcast(F32)
            return [[src[:, 512 * e + 128 * s : 512 * e + 128 * s + 128] for s in range(4)] for e in range(2)]

        def front_nf(g, halves=(0, 1), on_vector=()):
            if g not in nf_g:
                grouped = nfg_pool.tile([P, 4096], BF16, tag="nfg", align_bytes=64)
                nf_g[g] = grouped
            for half in halves:
                transposes(nf_words(g, half), nf_g[g], 2 * half, on_vector)

        def front_cv(i, on_vector=()):
            src = cv_raw[i][:].bitcast(F32)
            grouped = cvg_pool.tile([P, 4096], BF16, tag="cvg", align_bytes=64)
            words = [[src[:, 512 * b + 128 * s : 512 * b + 128 * s + 128] for s in range(4)] for b in range(4)]
            transposes(words, grouped, 0, on_vector)
            return grouped

        def stay_warm(count):
            idle = ps_m.tile([P, 512], F32, tag="mm")
            for n in range(count):
                nc.tensor.matmul(out=idle[:], lhsT=busy[:, 0:P], rhs=busy[:], start=True, stop=True)

        def open_nf(g):
            hg = hg_pool.tile([P, 4 * C_H], BF16, tag="hg", align_bytes=64)
            hgs[g] = hg
            accs = []
            for cb in range(4):
                acc = ps_m.tile([P, 512], F32, tag="mm")
                accs.append(acc)
            return accs

        def back_nf(g, accs, cbs=(0, 1, 2, 3), ues=(0, 1, 2, 3)):
            codes, scales = nf_q[g]
            for cb in cbs:
                acc = accs[cb]
                for ue in ues:
                    for kp in range(2):
                        m_cols = slice(128 * (2 * ue + kp), 128 * (2 * ue + kp) + 128)
                        n_cols = slice(512 * kp + 128 * cb, 512 * kp + 128 * cb + 128)
                        nc.tensor.matmul_mx(
                            out=acc[:, 128 * ue : 128 * ue + 128],
                            lhsT=codes[:, m_cols].bitcast(FP8X4),
                            lhsT_scale=scales[:, m_cols],
                            rhs=w1_codes[:, n_cols].bitcast(FP8X4),
                            rhs_scale=w1_scales[:, n_cols],
                            start=(kp == 0),
                            stop=(kp == 1),
                        )

        def add_bias(g, accs, cbs=(0, 1, 2, 3)):
            hg = hgs[g]
            for cb in cbs:
                acc = accs[cb]
                dst = hg[:, 512 * cb : 512 * cb + 512].rearrange("p (c t) -> p c t", t=4)
                prod = acc[:].rearrange("p (t c) -> p c t", t=4)
                bias_c = bias[:, 128 * cb : 128 * cb + 128].unsqueeze(2).to_broadcast([P, 128, 4])
                if (g, cb) in GPSIMD_ADDS:
                    hs = gp_pool.tile([P, 128, 4], F32, tag="hs")
                    nc.scalar.copy(out=hs[:], in_=prod)
                    nc.gpsimd.tensor_tensor(out=dst, in0=hs[:], in1=bias_c, op=ALU.add)
                else:
                    nc.vector.tensor_tensor(out=dst, in0=prod, in1=bias_c, op=ALU.add)

        def quant_h(g):
            hg = hgs[g]
            cols = slice(C_H * g, C_H * g + C_H)
            nc.vector.quantize_mx(out=h_codes[:, cols].bitcast(FP8X4), scales=h_scales[:, cols], in_=hg[:])

        def open_cv(i):
            pieces = []
            for a in range(2):
                width = LAST_WIDTH if (i, a) == (7, 1) else C_H
                for c0 in range(0, C_H, width):
                    if i == 7:
                        z = ps_t.tile([P, 512], F32, tag="tp")
                    else:
                        z = ps_m.tile([P, 512], F32, tag="mm")
                    pieces.append((a, slice(c0, c0 + width), z[:, 0:width]))
            return pieces

        def back_cv(i, pieces, gs=(0, 1, 2, 3)):
            codes, scales = cv_q[i]
            for a, cols, z in pieces:
                for g in gs:
                    m_cols = slice(128 * (4 * a + g), 128 * (4 * a + g) + 128)
                    n_cols = slice(C_H * g + cols.start, C_H * g + cols.stop)
                    nc.tensor.matmul_mx(
                        out=z,
                        lhsT=codes[:, m_cols].bitcast(FP8X4),
                        lhsT_scale=scales[:, m_cols],
                        rhs=h_codes[:, n_cols].bitcast(FP8X4),
                        rhs_scale=h_scales[:, n_cols],
                        start=(g == 0),
                        stop=(g == 3),
                    )

        def polynomial(i, pieces):
            res = res_pool.tile([P, 2, C_H], F32, tag="res")
            out_rows = out[256 * i : 256 * i + 256, :].rearrange("(p a) c -> p a c", a=2)
            first = []
            last = []
            late = []
            for a, cols, z in pieces:
                width = cols.stop - cols.start
                dst = res[:, a, cols]
                if (i, a) in GPSIMD_TILES:
                    zc = gp_pool.tile([P, 512], F32, tag="zc")
                    nc.scalar.copy(out=zc[:], in_=z)
                    tg = gp_pool.tile([P, 512], F32, tag="tg")
                    nc.gpsimd.tensor_scalar(
                        out=tg[:], in0=zc[:], scalar1=coef[:, 2:3], scalar2=coef[:, 1:2], op0=ALU.mult, op1=ALU.add
                    )
                    nc.gpsimd.tensor_tensor(out=tg[:], in0=tg[:], in1=zc[:], op=ALU.mult)
                    nc.gpsimd.tensor_scalar(
                        out=tg[:], in0=tg[:], scalar1=unit[:, 0:1], scalar2=coef[:, 0:1], op0=ALU.mult, op1=ALU.add
                    )
                    nc.gpsimd.tensor_tensor(out=dst, in0=tg[:], in1=zc[:], op=ALU.mult)
                    late.append((a, cols))
                elif (i, a) == (7, 0):
                    sq = poly_pool.tile([P, 512], F32, tag="sq", bufs=1)
                    nc.scalar.activation(out=sq[:], in_=z, func=ACT.Square)
                    t = poly_pool.tile([P, 512], F32, tag="t")
                    nc.scalar.activation(out=t[:], in_=z, func=ACT.Identity, scale=coef[:, 2:3], bias=coef[:, 1:2])
                    nc.gpsimd.tensor_tensor(out=t[:], in0=t[:], in1=sq[:], op=ALU.mult)
                    shared = (a, cols, (dst, z, t))
                else:
                    t = poly_pool.tile([P, 512], F32, tag="t")
                    nc.scalar.activation(out=t[:, 0:width], in_=z, func=ACT.Identity, scale=coef[:, 2:3])
                    first.append((t[:, 0:width], z))
                    last.append((a, cols, (dst, t[:, 0:width], z)))

            def store(a, cols):
                nc.sync.dma_start(out=out_rows[:, a, cols], in_=res[:, a, cols])

            def second(t, z):
                nc.vector.scalar_tensor_tensor(out=t, in0=t, scalar=coef[:, 1:2], in1=z, op0=ALU.add, op1=ALU.mult)

            def third(dst, t, z):
                nc.vector.scalar_tensor_tensor(out=dst, in0=t, scalar=coef[:, 0:1], in1=z, op0=ALU.add, op1=ALU.mult)

            if i == 7:
                second(*first[0])
                second(*first[1])
                third(*last[0][2])
                store(*last[0][:2])
                a, cols, (dst, z, t) = shared
                nc.vector.scalar_tensor_tensor(out=dst, in0=z, scalar=coef[:, 0:1], in1=t, op0=ALU.mult, op1=ALU.add)
                store(a, cols)
                third(*last[1][2])
                store(*last[1][:2])
            else:
                for t, z in first:
                    second(t, z)
                for a, cols, args in last:
                    third(*args)
                if len(last) == 2:
                    nc.sync.dma_start(out=out_rows, in_=res[:])
                else:
                    for a, cols, args in last:
                        store(a, cols)

            def finish():
                for a, cols in late:
                    store(a, cols)

            return finish

        nf_g = {}
        nf_q = {}
        cv_g = {}
        cv_q = {}
        hgs = {}
        ALL = (0, 1, 2, 3)
        stay_warm(4)
        front_nf(0, (0,))
        stay_warm(5)
        bias_ps = ps_t.tile([P, 512], F32, tag="tp")
        coef_ps = ps_t.tile([P, 512], F32, tag="tp")
        nc.tensor.matmul(out=bias_ps[:], lhsT=ones[:], rhs=row[:, 0:C_H], start=True, stop=True)
        nc.tensor.matmul(out=coef_ps[:, 0:32], lhsT=ones[:], rhs=row[:, C_H : C_H + 32], start=True, stop=True)
        codes0 = nfc_pool.tile([P, 1024], U32, tag="nfc", align_bytes=64)
        scales0 = nfc_pool.tile([P, 1024], U8, tag="nfs", align_bytes=64)
        nf_q[0] = (codes0, scales0)

        def quantise_nf0(half):
            cols = slice(512 * half, 512 * half + 512)
            nc.vector.quantize_mx(
                out=codes0[:, cols].bitcast(FP8X4),
                scales=scales0[:, cols],
                in_=nf_g[0][:, 2048 * half : 2048 * half + 2048],
            )

        left = slice(0, 256)
        right = slice(256, 512)
        regroup_w1(0, left, nc.vector.tensor_copy)
        regroup_w1(0, right, nc.scalar.copy)
        quantise_nf0(0)
        regroup_w1(1, left, nc.vector.tensor_copy)
        regroup_w1(1, right, nc.scalar.copy)
        quantise_w1(0, left)
        quantise_w1(1, left)
        nc.scalar.copy(out=bias[:], in_=bias_ps[:])
        nc.scalar.copy(out=coef[:], in_=coef_ps[:, 0:32])
        front_nf(0, (1,))
        quantise_w1(0, right)
        quantise_w1(1, right)
        accs = open_nf(0)
        back_nf(0, accs, ues=(0, 1))
        quantise_nf0(1)
        front_nf(1)
        back_nf(0, accs, ues=(2, 3))
        add_bias(0, accs, (0, 1))
        nf_q[1] = quantise(nf_g[1], nfc_pool, "nf")
        add_bias(0, accs, (2, 3))
        for g in (1, 2, 3):
            if g < 3:
                front_nf(g + 1)
            else:
                cv_g[0] = front_cv(0)
            accs = open_nf(g)
            back_nf(g, accs)
            quant_h(g - 1)
            if g < 3:
                nf_q[g + 1] = quantise(nf_g[g + 1], nfc_pool, "nf")
                add_bias(g, accs)
            else:
                add_bias(g, accs, (0,))
                cv_q[0] = quantise(cv_g[0], cvc_pool, "cv")
                add_bias(g, accs, (1, 2, 3))
        cv_g[1] = front_cv(1)
        quant_h(3)
        cv_q[1] = quantise(cv_g[1], cvc_pool, "cv")
        finish = None
        for i in range(8):
            pieces = open_cv(i)
            if i == 0:
                back_cv(i, pieces, (0, 1, 2))
                cv_g[2] = front_cv(2, (3,))
                back_cv(i, pieces, (3,))
            else:
                back_cv(i, pieces)
            finish_next = polynomial(i, pieces)
            if i == 0:
                cv_q[2] = quantise(cv_g[2], cvc_pool, "cv")
            if finish is not None:
                finish()
            finish = finish_next
            if i + LOOKAHEAD < 8:
                cv_g[i + LOOKAHEAD] = front_cv(i + LOOKAHEAD)
                cv_q[i + LOOKAHEAD] = quantise(cv_g[i + LOOKAHEAD], cvc_pool, "cv")
